import numpy as np
import ml_dtypes


def mxq(x, axis, fmt="e4m3"):
    dtype, down = {"e4m3": (ml_dtypes.float8_e4m3fn, 7), "e5m2": (ml_dtypes.float8_e5m2, 14)}[fmt]
    v = np.moveaxis(np.asarray(x, np.float32).astype(ml_dtypes.bfloat16).astype(np.float64), axis, -1)
    blocks = v.reshape(v.shape[:-1] + (-1, 32))
    amax = np.abs(blocks).max(-1, keepdims=True)
    byte = np.maximum(np.where(amax > 0, np.frexp(amax)[1] - 1 + 127, 0) - down, 1)
    scale = np.exp2(byte - 127.0)
    codes = (blocks / scale).astype(np.float32).astype(dtype).astype(np.float64)
    return np.moveaxis((codes * scale).reshape(v.shape), -1, axis)


WIDE = False


def mx_kscale(k):
    if not WIDE:
        return np.ones(k)
    levels = np.array([10, -10, 5, -5, 0])
    a = np.random.permutation(np.resize(levels, k // 512 * 4)).reshape(k // 512, 4)
    idx = np.arange(k)
    return np.exp2(a[idx // 512, idx % 128 // 32])


BF16 = ml_dtypes.bfloat16


def bf(x):
    return np.asarray(x, np.float32).astype(BF16)


def f64(x):
    return np.asarray(x).astype(np.float64)


E2M1 = np.array([0.0, 0.5, 1.0, 1.5, 2.0, 3.0, 4.0, 6.0, -0.0, -0.5, -1.0, -1.5, -2.0, -3.0, -4.0, -6.0])


def pack_weight(w, fmt):
    k, n = w.shape
    w = f64(bf(w)).reshape(k // 32, 32, n)
    amax = np.abs(w).max(1)
    if fmt == "e4m3":
        byte = np.frexp(amax)[1] - 1 + 127 - 7
    else:
        mant, ex = np.frexp(amax / 6.0)
        byte = np.where(mant > 0.5, ex, ex - 1) + 127
    byte = np.clip(np.where(amax > 0, byte, 1), 1, 254)
    scaled = (w * np.exp2(127.0 - byte)[:, None, :]).reshape(k, n).astype(np.float32)
    by_word = np.ascontiguousarray(scaled.reshape(k // 512, 128, 4, n).transpose(0, 1, 3, 2))
    if fmt == "e4m3":
        words = by_word.astype(ml_dtypes.float8_e4m3fn).view(np.uint8)
    else:
        c = by_word.astype(ml_dtypes.float4_e2m1fn).view(np.uint8) & 0xF
        words = c[..., 0::2] | (c[..., 1::2] << 4)
    return np.ascontiguousarray(words), np.ascontiguousarray(byte.astype(np.uint8).reshape(k // 512, 16, n))


def unpack_weight(words, scales, fmt):
    g, p, n, _ = words.shape
    if fmt == "e4m3":
        vals = np.ascontiguousarray(words).view(ml_dtypes.float8_e4m3fn).astype(np.float64)
    else:
        nib = np.empty((g, p, n, 4), np.uint8)
        nib[..., 0::2] = words & 0xF
        nib[..., 1::2] = words >> 4
        vals = E2M1[nib]
    vals = vals * np.repeat(np.exp2(scales.astype(np.float64) - 127.0), 8, axis=1)[..., None]
    return vals.transpose(0, 1, 3, 2).reshape(g * 512, n)

def pack4(w):
    words, scales = pack_weight(w, "e2m1")
    return words.reshape(words.shape[0], 128, -1), scales


def unpack4(words, scales):
    return unpack_weight(words.reshape(words.shape[0], 128, -1, 2), scales, "e2m1")


B, IN, H = 256, 8192, 1024


def sigmoid(v):
    return 1.0 / (1.0 + np.exp(-v))


def setup_inputs():
    s = mx_kscale(IN)
    g = np.random.standard_normal((H, IN + H)) / np.sqrt(IN + H)
    g[:, :IN] /= s
    x = bf(np.random.standard_normal((B, IN)) * s)
    h = bf(np.random.standard_normal((B, H)))
    tau = bf(np.random.standard_normal(H))
    w_in = np.random.standard_normal((H, IN)) / np.sqrt(IN) / s
    w_rec = np.random.standard_normal((H, H)) * 1.5 / np.sqrt(H)
    gate_b = bf(np.random.standard_normal(H) * 0.5)
    W_in_words, W_in_scales = pack4(np.ascontiguousarray(w_in.T))
    W_rec_words, W_rec_scales = pack4(np.ascontiguousarray(w_rec.T))
    gate_w_words, gate_w_scales = pack4(np.ascontiguousarray(g.T))
    return {"x": x,
            "h": h,
            "tau": tau,
            "W_in_words": W_in_words,
            "W_in_scales": W_in_scales,
            "W_rec_words": W_rec_words,
            "W_rec_scales": W_rec_scales,
            "gate_w_words": gate_w_words,
            "gate_w_scales": gate_w_scales,
            "gate_b": gate_b}


def reference(x, h, tau, W_in_words, W_in_scales, W_rec_words, W_rec_scales, gate_w_words, gate_w_scales, gate_b):
    tau_p = np.log(1.0 + np.exp(f64(tau))) + 1.0
    gt = unpack4(gate_w_words, gate_w_scales)
    xq = mxq(f64(x), 1, "e4m3")
    hq = mxq(f64(h), 1, "e4m3")
    x_in = xq @ unpack4(W_in_words, W_in_scales)
    pre = (xq @ gt[:IN]) + (hq @ gt[IN:]) + f64(gate_b)
    gate = sigmoid(np.tanh(pre))
    k1 = -f64(h) / tau_p + x_in + gate * (hq @ unpack4(W_rec_words, W_rec_scales))
    return x_in, k1

@@ -1,0 +1,318 @@
+import concourse.mybir as mybir
+from concourse.masks import make_identity
+
+F32 = mybir.dt.float32
+BF16 = mybir.dt.bfloat16
+I32 = mybir.dt.int32
+U32 = mybir.dt.uint32
+U8 = mybir.dt.uint8
+FP8X4 = mybir.dt.float8_e4m3fn_x4
+FP4X4 = mybir.dt.float4_e2m1fn_x4
+ACT = mybir.ActivationFunctionType
+ALU = mybir.AluOpType
+
+P = 128
+B, IN, H = 256, 8192, 1024
+K_PASS = 4 * P
+N_PASS = 512
+ROW_TILES = B // P
+COL_HALVES = H // N_PASS
+X_GROUPS = IN // K_PASS
+H_GROUPS = H // K_PASS
+PAIR = 2
+STAGE = 4
+X_STAGES = X_GROUPS // STAGE
+WORDS = K_PASS // 2
+WEIGHT_BUFFERS = 12
+
+FLOPS = 2 * B * (2 * IN * H + 2 * H * H)
+
+
+def bank_columns(half):
+    return slice(half * N_PASS, (half + 1) * N_PASS)
+
+
+def zero_planes(nc, planes):
+    nc.vector.memset(planes.bitcast(I32), 0)
+
+
+def load_scale_rows(nc, planes, scales, first, count):
+    groups = slice(first, first + count)
+    for q in range(8):
+        partition = 32 * (q // 4) + q % 4
+        nc.sync.dma_start(
+            out=planes[partition:P:64, groups, :].bitcast(I32),
+            in_=scales[groups, q:16:8, :].bitcast(I32).rearrange("g q n -> q g n"),
+        )
+
+
+def load_weight_pair(nc, pool, words, pair, name):
+    tile = pool.tile([P, PAIR, 2 * H], U8, tag="words", name=name, align_bytes=64)
+    nc.sync.dma_start(
+        out=tile[:].bitcast(I32),
+        in_=words[PAIR * pair : PAIR * (pair + 1)].bitcast(I32).rearrange("g p n -> p g n"),
+    )
+    return tile
+
+
+def transpose_and_quantise(nc, banks, regroup, ident, raw, groups, codes, code_scales, first):
+    raw_words = raw[:].bitcast(F32)
+    grouped = regroup.tile([P, groups, 4 * B], BF16, tag="grouped", align_bytes=64)
+    for g in range(groups):
+        bank = banks.tile([P, N_PASS], F32, tag="bank", name="transposed")
+        for b in range(ROW_TILES):
+            for u in range(2):
+                nc.tensor.transpose(
+                    bank[:, (2 * b + u) * P : (2 * b + u + 1) * P],
+                    raw_words[:, b, g * WORDS + u : (g + 1) * WORDS : 2],
+                    ident[:],
+                )
+        copy = nc.vector.tensor_copy if g % 2 == 0 else nc.scalar.copy
+        copy(
+            out=grouped[:, g, :].bitcast(F32).rearrange("p (b r u) -> p b r u", b=ROW_TILES, u=2),
+            in_=bank[:].rearrange("p (b u r) -> p b r u", b=ROW_TILES, u=2),
+        )
+    for g in range(0, groups, PAIR):
+        slots = slice(first + g, first + g + PAIR)
+        nc.vector.quantize_mx(
+            out=codes[:, slots, :].rearrange("p g c -> p (g c)").bitcast(FP8X4),
+            scales=code_scales[:, slots, :].rearrange("p g c -> p (g c)"),
+            in_=grouped[:, g : g + PAIR, :].rearrange("p g c -> p (g c)"),
+        )
+
+
+def multiply_pair(nc, acc, codes, code_scales, slot, words, planes, group, start, stop):
+    for b in range(ROW_TILES):
+        rows = slice(b * P, (b + 1) * P)
+        for half in range(COL_HALVES):
+            for i in range(PAIR):
+                nc.tensor.matmul_mx(
+                    out=acc[b][half][:],
+                    lhsT=codes[:, slot + i, rows].bitcast(FP8X4),
+                    lhsT_scale=code_scales[:, slot + i, rows],
+                    rhs=words[:, i, 2 * half * N_PASS : 2 * (half + 1) * N_PASS].bitcast(FP4X4),
+                    rhs_scale=planes[:, group + i, bank_columns(half)],
+                    start=start and i == 0,
+                    stop=stop and i == PAIR - 1,
+                )
+
+
+def tile_ltccell_pa_k_kernel(
+    tc,
+    x,
+    h,
+    tau,
+    W_in_words,
+    W_in_scales,
+    W_rec_words,
+    W_rec_scales,
+    gate_w_words,
+    gate_w_scales,
+    gate_b,
+    out_0,
+    out_1,
+):
+    nc = tc.nc
+    x_rows = x.rearrange("(b p) k -> p b k", p=P)
+    h_rows = h.rearrange("(b p) k -> p b k", p=P)
+
+    with (
+        tc.tile_pool(name="keep", bufs=1) as keep,
+        tc.tile_pool(name="weights", bufs=WEIGHT_BUFFERS) as weights,
+        tc.tile_pool(name="regroup", bufs=2) as regroup,
+        tc.tile_pool(name="work", bufs=ROW_TILES * COL_HALVES) as work,
+        tc.psum_pool(name="banks", bufs=4) as banks,
+        tc.psum_pool(name="sums", bufs=4) as sums,
+        tc.manual_schedule(),
+    ):
+        ident = keep.tile([P, P], F32)
+        make_identity(nc, ident[:])
+        ones = keep.tile([P, P], BF16)
+        nc.gpsimd.memset(ones[:], 1.0)
+        vectors = keep.tile([P, 2 * H], BF16)
+        nc.gpsimd.memset(vectors[:], 0.0)
+        nc.scalar.dma_start(out=vectors[0:1, 0:H], in_=tau.rearrange("(o n) -> o n", o=1))
+        nc.scalar.dma_start(out=vectors[0:1, H : 2 * H], in_=gate_b.rearrange("(o n) -> o n", o=1))
+
+        rec_planes = keep.tile([P, H_GROUPS, H], U8, align_bytes=64)
+        gate_planes = keep.tile([P, X_GROUPS + H_GROUPS, H], U8, align_bytes=64)
+        in_planes = keep.tile([P, X_GROUPS, H], U8, align_bytes=64)
+        zero_planes(nc, rec_planes[:])
+        zero_planes(nc, gate_planes[:, X_GROUPS:, :])
+        for s in range(X_STAGES):
+            zero_planes(nc, gate_planes[:, s * STAGE : (s + 1) * STAGE, :])
+        for s in range(X_STAGES):
+            zero_planes(nc, in_planes[:, s * STAGE : (s + 1) * STAGE, :])
+
+        def load_x_stage(s):
+            tile = keep.tile([P, ROW_TILES, STAGE * K_PASS], BF16, name="x_raw%d" % s)
+            columns = slice(s * STAGE * K_PASS, (s + 1) * STAGE * K_PASS)
+            nc.sync.dma_start(out=tile[:], in_=x_rows[:, :, columns])
+            return tile
+
+        h_raw = keep.tile([P, ROW_TILES, H], BF16)
+        nc.sync.dma_start(out=h_raw[:], in_=h_rows)
+        x_raw = [load_x_stage(0)]
+        load_scale_rows(nc, rec_planes, W_rec_scales, 0, H_GROUPS)
+        load_scale_rows(nc, gate_planes, gate_w_scales, X_GROUPS, H_GROUPS)
+        rec_words = load_weight_pair(nc, weights, W_rec_words, 0, "rec_words")
+        gate_h_words = load_weight_pair(nc, weights, gate_w_words, X_GROUPS // PAIR, "gate_h_words")
+        gate_words = []
+        for s in range(X_STAGES):
+            if s + 1 < X_STAGES:
+                x_raw.append(load_x_stage(s + 1))
+            load_scale_rows(nc, gate_planes, gate_w_scales, s * STAGE, STAGE)
+            for pair in range(s * STAGE // PAIR, (s + 1) * STAGE // PAIR):
+                gate_words.append(load_weight_pair(nc, weights, gate_w_words, pair, "gate_words"))
+        in_words = []
+        for s in range(X_STAGES):
+            load_scale_rows(nc, in_planes, W_in_scales, s * STAGE, STAGE)
+            for pair in range(s * STAGE // PAIR, (s + 1) * STAGE // PAIR):
+                in_words.append(load_weight_pair(nc, weights, W_in_words, pair, "in_words"))
+
+        codes = keep.tile([P, X_GROUPS + H_GROUPS, B], U32, align_bytes=64)
+        code_scales = keep.tile([P, X_GROUPS + H_GROUPS, B], U8, align_bytes=64)
+
+        def quantise_x_stage(s):
+            transpose_and_quantise(
+                nc, banks, regroup, ident, x_raw[s], STAGE, codes, code_scales, s * STAGE
+            )
+
+        transpose_and_quantise(
+            nc, banks, regroup, ident, h_raw, H_GROUPS, codes, code_scales, X_GROUPS
+        )
+        quantise_x_stage(0)
+
+        tau_all = keep.tile([P, H], F32)
+        bias_all = keep.tile([P, H], F32)
+        for half in range(COL_HALVES):
+            spread_tau = banks.tile([P, N_PASS], F32, tag="bank")
+            nc.tensor.matmul(
+                spread_tau[:], lhsT=ones[:], rhs=vectors[:, bank_columns(half)], start=True, stop=True
+            )
+            nc.scalar.copy(out=tau_all[:, bank_columns(half)], in_=spread_tau[:])
+            spread_bias = banks.tile([P, N_PASS], F32, tag="bank")
+            nc.tensor.matmul(
+                spread_bias[:],
+                lhsT=ones[:],
+                rhs=vectors[:, H + half * N_PASS : H + (half + 1) * N_PASS],
+                start=True,
+                stop=True,
+            )
+            nc.vector.tensor_copy(out=bias_all[:, bank_columns(half)], in_=spread_bias[:])
+
+        def four_banks(pool, name):
+            return [
+                [
+                    pool.tile([P, N_PASS], F32, tag="bank", name="%s%d%d" % (name, b, half))
+                    for half in range(COL_HALVES)
+                ]
+                for b in range(ROW_TILES)
+            ]
+
+        rec_acc = four_banks(sums, "rec_acc")
+        multiply_pair(
+            nc, rec_acc, codes, code_scales, X_GROUPS, rec_words, rec_planes, 0, True, True
+        )
+        rec = keep.tile([P, ROW_TILES, H], F32)
+        for b in range(ROW_TILES):
+            nc.vector.tensor_copy(out=rec[:, b, bank_columns(0)], in_=rec_acc[b][0][:])
+            nc.scalar.copy(out=rec[:, b, bank_columns(1)], in_=rec_acc[b][1][:])
+
+        pre_acc = four_banks(sums, "pre_acc")
+        multiply_pair(
+            nc, pre_acc, codes, code_scales, X_GROUPS, gate_h_words, gate_planes, X_GROUPS, True, False
+        )
+        quantise_x_stage(1)
+
+        tau_p = keep.tile([P, H], F32)
+        nc.scalar.activation(out=tau_p[:], in_=tau_all[:], func=ACT.Abs)
+        nc.scalar.activation(out=tau_p[:], in_=tau_p[:], func=ACT.Exp, scale=-1.0)
+        nc.scalar.activation(out=tau_p[:], in_=tau_p[:], func=ACT.Ln, bias=1.0)
+        nc.vector.tensor_scalar_max(out=tau_all[:], in0=tau_all[:], scalar1=0.0)
+        nc.vector.scalar_tensor_tensor(
+            out=tau_p[:], in0=tau_p[:], scalar=1.0, in1=tau_all[:], op0=ALU.add, op1=ALU.add
+        )
+
+        for s in range(X_STAGES):
+            for pair in range(s * STAGE // PAIR, (s + 1) * STAGE // PAIR):
+                multiply_pair(
+                    nc,
+                    pre_acc,
+                    codes,
+                    code_scales,
+                    pair * PAIR,
+                    gate_words[pair],
+                    gate_planes,
+                    pair * PAIR,
+                    False,
+                    pair == X_GROUPS // PAIR - 1,
+                )
+            if s + 2 < X_STAGES:
+                quantise_x_stage(s + 2)
+            quarter = slice(s * H // X_STAGES, (s + 1) * H // X_STAGES)
+            nc.vector.reciprocal(out=tau_p[:, quarter], in_=tau_p[:, quarter])
+
+        rest = keep.tile([P, ROW_TILES, H], F32)
+        for b in range(ROW_TILES):
+            nc.vector.scalar_tensor_tensor(
+                out=rest[:, b, :],
+                in0=h_raw[:, b, :],
+                scalar=-1.0,
+                in1=tau_p[:],
+                op0=ALU.mult,
+                op1=ALU.mult,
+            )
+        all_banks = [(b, half) for b in range(ROW_TILES) for half in range(COL_HALVES)]
+        gate = {}
+        for b, half in all_banks:
+            gate[b, half] = work.tile([P, N_PASS], F32, tag="gate", name="gate")
+            nc.vector.tensor_tensor(
+                out=gate[b, half][:],
+                in0=pre_acc[b][half][:],
+                in1=bias_all[:, bank_columns(half)],
+                op=ALU.add,
+            )
+        for b, half in all_banks:
+            nc.scalar.activation(out=gate[b, half][:], in_=gate[b, half][:], func=ACT.Tanh)
+            nc.scalar.activation(out=gate[b, half][:], in_=gate[b, half][:], func=ACT.Sigmoid)
+        for b, half in all_banks:
+            nc.vector.tensor_tensor(
+                out=gate[b, half][:],
+                in0=gate[b, half][:],
+                in1=rec[:, b, bank_columns(half)],
+                op=ALU.mult,
+            )
+            nc.vector.tensor_tensor(
+                out=rest[:, b, bank_columns(half)],
+                in0=gate[b, half][:],
+                in1=rest[:, b, bank_columns(half)],
+                op=ALU.add,
+            )
+
+        in_acc = four_banks(banks, "in_acc")
+        for pair in range(X_GROUPS // PAIR):
+            multiply_pair(
+                nc,
+                in_acc,
+                codes,
+                code_scales,
+                pair * PAIR,
+                in_words[pair],
+                in_planes,
+                pair * PAIR,
+                pair == 0,
+                pair == X_GROUPS // PAIR - 1,
+            )
+        for b, half in all_banks:
+            rows = slice(b * P, (b + 1) * P)
+            x_in = work.tile([P, N_PASS], F32, tag="x_in")
+            nc.scalar.copy(out=x_in[:], in_=in_acc[b][half][:])
+            nc.sync.dma_start(out=out_0[rows, bank_columns(half)], in_=x_in[:])
+            nc.vector.tensor_tensor(
+                out=rest[:, b, bank_columns(half)],
+                in0=x_in[:],
+                in1=rest[:, b, bank_columns(half)],
+                op=ALU.add,
+            )
+            nc.sync.dma_start(out=out_1[rows, bank_columns(half)], in_=rest[:, b, bank_columns(half)])

@@ -17,12 +17,15 @@ K_PASS = 4 * P
 N_PASS = 512
 ROW_TILES = B // P
 COL_HALVES = H // N_PASS
+BANKS = [(b, half) for b in range(ROW_TILES) for half in range(COL_HALVES)]
 X_GROUPS = IN // K_PASS
 H_GROUPS = H // K_PASS
 PAIR = 2
+X_PAIRS = X_GROUPS // PAIR
 STAGE = 4
 X_STAGES = X_GROUPS // STAGE
 WORDS = K_PASS // 2
+GATE_RUN = 8
 WEIGHT_BUFFERS = 12
 
 FLOPS = 2 * B * (2 * IN * H + 2 * H * H)
@@ -32,17 +35,18 @@ def bank_columns(half):
     return slice(half * N_PASS, (half + 1) * N_PASS)
 
 
-def zero_planes(nc, planes):
-    nc.vector.memset(planes.bitcast(I32), 0)
+def scale_planes(nc, pool, groups, name):
+    planes = pool.tile([P, groups, H], U8, name=name, align_bytes=64)
+    nc.vector.memset(planes[:].bitcast(I32), 0)
+    return planes
 
 
 def load_scale_rows(nc, planes, scales, first, count):
-    groups = slice(first, first + count)
     for q in range(8):
         partition = 32 * (q // 4) + q % 4
         nc.sync.dma_start(
-            out=planes[partition:P:64, groups, :].bitcast(I32),
-            in_=scales[groups, q:16:8, :].bitcast(I32).rearrange("g q n -> q g n"),
+            out=planes[partition:P:64, :, :].bitcast(I32),
+            in_=scales[first : first + count, q:16:8, :].bitcast(I32).rearrange("g q n -> q g n"),
         )
 
 
@@ -55,46 +59,63 @@ def load_weight_pair(nc, pool, words, pair, name):
     return tile
 
 
-def transpose_and_quantise(nc, banks, regroup, ident, raw, groups, codes, code_scales, first):
+def transpose_and_quantise(nc, pools, ident, raw, groups, name):
+    keep, regroup, banks = pools
     raw_words = raw[:].bitcast(F32)
-    grouped = regroup.tile([P, groups, 4 * B], BF16, tag="grouped", align_bytes=64)
-    for g in range(groups):
-        bank = banks.tile([P, N_PASS], F32, tag="bank", name="transposed")
-        for b in range(ROW_TILES):
-            for u in range(2):
-                nc.tensor.transpose(
-                    bank[:, (2 * b + u) * P : (2 * b + u + 1) * P],
-                    raw_words[:, b, g * WORDS + u : (g + 1) * WORDS : 2],
-                    ident[:],
-                )
-        copy = nc.vector.tensor_copy if g % 2 == 0 else nc.scalar.copy
-        copy(
-            out=grouped[:, g, :].bitcast(F32).rearrange("p (b r u) -> p b r u", b=ROW_TILES, u=2),
-            in_=bank[:].rearrange("p (b u r) -> p b r u", b=ROW_TILES, u=2),
-        )
-    for g in range(0, groups, PAIR):
-        slots = slice(first + g, first + g + PAIR)
+    grouped = []
+    for pair in range(groups // PAIR):
+        grouped.append(regroup.tile([P, PAIR, 4 * B], BF16, tag="grouped", name="grouped", align_bytes=64))
+        for i in range(PAIR):
+            g = pair * PAIR + i
+            bank = banks.tile([P, N_PASS], F32, tag="bank", name="transposed")
+            for b in range(ROW_TILES):
+                for u in range(2):
+                    nc.tensor.transpose(
+                        bank[:, (2 * b + u) * P : (2 * b + u + 1) * P],
+                        raw_words[:, b, g * WORDS + u : (g + 1) * WORDS : 2],
+                        ident[:],
+                    )
+            copy = nc.vector.tensor_copy if i == 0 else nc.scalar.copy
+            copy(
+                out=grouped[pair][:, i, :]
+                .bitcast(F32)
+                .rearrange("p (b r u) -> p b r u", b=ROW_TILES, u=2),
+                in_=bank[:].rearrange("p (b u r) -> p b r u", b=ROW_TILES, u=2),
+            )
+    quantised = []
+    for pair in range(groups // PAIR):
+        codes = keep.tile([P, PAIR, B], U32, name="%s_codes%d" % (name, pair), align_bytes=64)
+        scales = keep.tile([P, PAIR, B], U8, name="%s_scales%d" % (name, pair), align_bytes=64)
         nc.vector.quantize_mx(
-            out=codes[:, slots, :].rearrange("p g c -> p (g c)").bitcast(FP8X4),
-            scales=code_scales[:, slots, :].rearrange("p g c -> p (g c)"),
-            in_=grouped[:, g : g + PAIR, :].rearrange("p g c -> p (g c)"),
+            out=codes[:].rearrange("p g c -> p (g c)").bitcast(FP8X4),
+            scales=scales[:].rearrange("p g c -> p (g c)"),
+            in_=grouped[pair][:].rearrange("p g c -> p (g c)"),
         )
+        quantised.append((codes, scales))
+    return quantised
 
 
-def multiply_pair(nc, acc, codes, code_scales, slot, words, planes, group, start, stop):
-    for b in range(ROW_TILES):
+def multiply_pair(nc, acc, quantised, words, planes, group, start, stop):
+    codes, scales = quantised
+    for b, half in BANKS:
         rows = slice(b * P, (b + 1) * P)
-        for half in range(COL_HALVES):
-            for i in range(PAIR):
-                nc.tensor.matmul_mx(
-                    out=acc[b][half][:],
-                    lhsT=codes[:, slot + i, rows].bitcast(FP8X4),
-                    lhsT_scale=code_scales[:, slot + i, rows],
-                    rhs=words[:, i, 2 * half * N_PASS : 2 * (half + 1) * N_PASS].bitcast(FP4X4),
-                    rhs_scale=planes[:, group + i, bank_columns(half)],
-                    start=start and i == 0,
-                    stop=stop and i == PAIR - 1,
-                )
+        for i in range(PAIR):
+            nc.tensor.matmul_mx(
+                out=acc[b, half][:],
+                lhsT=codes[:, i, rows].bitcast(FP8X4),
+                lhsT_scale=scales[:, i, rows],
+                rhs=words[:, i, 2 * half * N_PASS : 2 * (half + 1) * N_PASS].bitcast(FP4X4),
+                rhs_scale=planes[:, group + i, bank_columns(half)],
+                start=start and i == 0,
+                stop=stop and i == PAIR - 1,
+            )
+
+
+def four_tiles(pool, tag, name):
+    return dict(
+        ((b, half), pool.tile([P, N_PASS], F32, tag=tag, name="%s%d%d" % (name, b, half)))
+        for b, half in BANKS
+    )
 
 
 def tile_ltccell_pa_k_kernel(
@@ -119,200 +140,173 @@ def tile_ltccell_pa_k_kernel(
     with (
         tc.tile_pool(name="keep", bufs=1) as keep,
         tc.tile_pool(name="weights", bufs=WEIGHT_BUFFERS) as weights,
-        tc.tile_pool(name="regroup", bufs=2) as regroup,
-        tc.tile_pool(name="work", bufs=ROW_TILES * COL_HALVES) as work,
+        tc.tile_pool(name="regroup", bufs=4) as regroup,
+        tc.tile_pool(name="work", bufs=len(BANKS)) as work,
         tc.psum_pool(name="banks", bufs=4) as banks,
         tc.psum_pool(name="sums", bufs=4) as sums,
         tc.manual_schedule(),
     ):
-        ident = keep.tile([P, P], F32)
-        make_identity(nc, ident[:])
-        ones = keep.tile([P, P], BF16)
-        nc.gpsimd.memset(ones[:], 1.0)
+        gate_planes = [scale_planes(nc, keep, GATE_RUN, "gate_planes0")]
         vectors = keep.tile([P, 2 * H], BF16)
-        nc.gpsimd.memset(vectors[:], 0.0)
+        nc.vector.memset(vectors[:].bitcast(I32), 0)
         nc.scalar.dma_start(out=vectors[0:1, 0:H], in_=tau.rearrange("(o n) -> o n", o=1))
         nc.scalar.dma_start(out=vectors[0:1, H : 2 * H], in_=gate_b.rearrange("(o n) -> o n", o=1))
+        ones = keep.tile([P, P], BF16)
+        nc.vector.memset(ones[:], 1.0)
+        gate_planes.append(
+            scale_planes(nc, keep, X_GROUPS + H_GROUPS - GATE_RUN, "gate_planes1")
+        )
+        rec_planes = scale_planes(nc, keep, H_GROUPS, "rec_planes")
+        in_planes = scale_planes(nc, keep, X_GROUPS, "in_planes")
+        ident = keep.tile([P, P], F32)
+        make_identity(nc, ident[:])
 
-        rec_planes = keep.tile([P, H_GROUPS, H], U8, align_bytes=64)
-        gate_planes = keep.tile([P, X_GROUPS + H_GROUPS, H], U8, align_bytes=64)
-        in_planes = keep.tile([P, X_GROUPS, H], U8, align_bytes=64)
-        zero_planes(nc, rec_planes[:])
-        zero_planes(nc, gate_planes[:, X_GROUPS:, :])
-        for s in range(X_STAGES):
-            zero_planes(nc, gate_planes[:, s * STAGE : (s + 1) * STAGE, :])
-        for s in range(X_STAGES):
-            zero_planes(nc, in_planes[:, s * STAGE : (s + 1) * STAGE, :])
-
-        def load_x_stage(s):
-            tile = keep.tile([P, ROW_TILES, STAGE * K_PASS], BF16, name="x_raw%d" % s)
-            columns = slice(s * STAGE * K_PASS, (s + 1) * STAGE * K_PASS)
-            nc.sync.dma_start(out=tile[:], in_=x_rows[:, :, columns])
+        def load_rows(rows, first, count, name):
+            tile = keep.tile([P, ROW_TILES, count * K_PASS], BF16, name=name)
+            nc.sync.dma_start(
+                out=tile[:], in_=rows[:, :, first * K_PASS : (first + count) * K_PASS]
+            )
             return tile
 
-        h_raw = keep.tile([P, ROW_TILES, H], BF16)
-        nc.sync.dma_start(out=h_raw[:], in_=h_rows)
-        x_raw = [load_x_stage(0)]
-        load_scale_rows(nc, rec_planes, W_rec_scales, 0, H_GROUPS)
-        load_scale_rows(nc, gate_planes, gate_w_scales, X_GROUPS, H_GROUPS)
-        rec_words = load_weight_pair(nc, weights, W_rec_words, 0, "rec_words")
-        gate_h_words = load_weight_pair(nc, weights, gate_w_words, X_GROUPS // PAIR, "gate_h_words")
+        raw = [load_rows(x_rows, 0, STAGE, "x_raw0")]
         gate_words = []
         for s in range(X_STAGES):
+            if s * STAGE == 0:
+                load_scale_rows(nc, gate_planes[0], gate_w_scales, 0, GATE_RUN)
+            if s * STAGE == GATE_RUN:
+                load_scale_rows(
+                    nc, gate_planes[1], gate_w_scales, GATE_RUN, X_GROUPS + H_GROUPS - GATE_RUN
+                )
+                load_scale_rows(nc, rec_planes, W_rec_scales, 0, H_GROUPS)
+            gate_words.append(load_weight_pair(nc, weights, gate_w_words, 2 * s, "gate_words"))
             if s + 1 < X_STAGES:
-                x_raw.append(load_x_stage(s + 1))
-            load_scale_rows(nc, gate_planes, gate_w_scales, s * STAGE, STAGE)
-            for pair in range(s * STAGE // PAIR, (s + 1) * STAGE // PAIR):
-                gate_words.append(load_weight_pair(nc, weights, gate_w_words, pair, "gate_words"))
-        in_words = []
-        for s in range(X_STAGES):
-            load_scale_rows(nc, in_planes, W_in_scales, s * STAGE, STAGE)
-            for pair in range(s * STAGE // PAIR, (s + 1) * STAGE // PAIR):
-                in_words.append(load_weight_pair(nc, weights, W_in_words, pair, "in_words"))
+                raw.append(load_rows(x_rows, (s + 1) * STAGE, STAGE, "x_raw%d" % (s + 1)))
+            else:
+                raw.append(load_rows(h_rows, 0, H_GROUPS, "h_raw"))
+            gate_words.append(load_weight_pair(nc, weights, gate_w_words, 2 * s + 1, "gate_words"))
+        gate_words.append(load_weight_pair(nc, weights, gate_w_words, X_PAIRS, "gate_words"))
+        rec_words = load_weight_pair(nc, weights, W_rec_words, 0, "rec_words")
+        load_scale_rows(nc, in_planes, W_in_scales, 0, X_GROUPS)
+        in_words = [
+            load_weight_pair(nc, weights, W_in_words, pair, "in_words") for pair in range(X_PAIRS)
+        ]
+        h_raw = raw[X_STAGES]
 
-        codes = keep.tile([P, X_GROUPS + H_GROUPS, B], U32, align_bytes=64)
-        code_scales = keep.tile([P, X_GROUPS + H_GROUPS, B], U8, align_bytes=64)
+        pools = (keep, regroup, banks)
+        quantised = transpose_and_quantise(nc, pools, ident, raw[0], STAGE, "x0")
 
-        def quantise_x_stage(s):
-            transpose_and_quantise(
-                nc, banks, regroup, ident, x_raw[s], STAGE, codes, code_scales, s * STAGE
-            )
-
-        transpose_and_quantise(
-            nc, banks, regroup, ident, h_raw, H_GROUPS, codes, code_scales, X_GROUPS
-        )
-        quantise_x_stage(0)
-
-        tau_all = keep.tile([P, H], F32)
+        spread = four_tiles(sums, "bank", "spread")
+        relu_tau = keep.tile([P, H], F32)
+        log_term = keep.tile([P, H], F32)
         bias_all = keep.tile([P, H], F32)
-        for half in range(COL_HALVES):
-            spread_tau = banks.tile([P, N_PASS], F32, tag="bank")
+        for vector, half in BANKS:
             nc.tensor.matmul(
-                spread_tau[:], lhsT=ones[:], rhs=vectors[:, bank_columns(half)], start=True, stop=True
-            )
-            nc.scalar.copy(out=tau_all[:, bank_columns(half)], in_=spread_tau[:])
-            spread_bias = banks.tile([P, N_PASS], F32, tag="bank")
-            nc.tensor.matmul(
-                spread_bias[:],
+                spread[vector, half][:],
                 lhsT=ones[:],
-                rhs=vectors[:, H + half * N_PASS : H + (half + 1) * N_PASS],
+                rhs=vectors[:, vector * H + half * N_PASS : vector * H + (half + 1) * N_PASS],
                 start=True,
                 stop=True,
             )
-            nc.vector.tensor_copy(out=bias_all[:, bank_columns(half)], in_=spread_bias[:])
+        for half in range(COL_HALVES):
+            nc.scalar.activation(
+                out=log_term[:, bank_columns(half)], in_=spread[0, half][:], func=ACT.Abs
+            )
+            nc.scalar.activation(
+                out=relu_tau[:, bank_columns(half)], in_=spread[0, half][:], func=ACT.Relu
+            )
+            nc.vector.tensor_copy(out=bias_all[:, bank_columns(half)], in_=spread[1, half][:])
+        nc.scalar.activation(out=log_term[:], in_=log_term[:], func=ACT.Exp, scale=-1.0)
+        nc.scalar.activation(out=log_term[:], in_=log_term[:], func=ACT.Ln, bias=1.0)
 
-        def four_banks(pool, name):
-            return [
-                [
-                    pool.tile([P, N_PASS], F32, tag="bank", name="%s%d%d" % (name, b, half))
-                    for half in range(COL_HALVES)
-                ]
-                for b in range(ROW_TILES)
-            ]
-
-        rec_acc = four_banks(sums, "rec_acc")
-        multiply_pair(
-            nc, rec_acc, codes, code_scales, X_GROUPS, rec_words, rec_planes, 0, True, True
-        )
-        rec = keep.tile([P, ROW_TILES, H], F32)
-        for b in range(ROW_TILES):
-            nc.vector.tensor_copy(out=rec[:, b, bank_columns(0)], in_=rec_acc[b][0][:])
-            nc.scalar.copy(out=rec[:, b, bank_columns(1)], in_=rec_acc[b][1][:])
-
-        pre_acc = four_banks(sums, "pre_acc")
-        multiply_pair(
-            nc, pre_acc, codes, code_scales, X_GROUPS, gate_h_words, gate_planes, X_GROUPS, True, False
-        )
-        quantise_x_stage(1)
-
-        tau_p = keep.tile([P, H], F32)
-        nc.scalar.activation(out=tau_p[:], in_=tau_all[:], func=ACT.Abs)
-        nc.scalar.activation(out=tau_p[:], in_=tau_p[:], func=ACT.Exp, scale=-1.0)
-        nc.scalar.activation(out=tau_p[:], in_=tau_p[:], func=ACT.Ln, bias=1.0)
-        nc.vector.tensor_scalar_max(out=tau_all[:], in0=tau_all[:], scalar1=0.0)
-        nc.vector.scalar_tensor_tensor(
-            out=tau_p[:], in0=tau_p[:], scalar=1.0, in1=tau_all[:], op0=ALU.add, op1=ALU.add
-        )
-
+        pre_acc = four_tiles(sums, "bank", "pre_acc")
+        inv_tau_p = keep.tile([P, H], F32)
         for s in range(X_STAGES):
-            for pair in range(s * STAGE // PAIR, (s + 1) * STAGE // PAIR):
+            for pair in (2 * s, 2 * s + 1):
                 multiply_pair(
                     nc,
                     pre_acc,
-                    codes,
-                    code_scales,
-                    pair * PAIR,
+                    quantised[pair],
                     gate_words[pair],
-                    gate_planes,
-                    pair * PAIR,
+                    gate_planes[pair * PAIR // GATE_RUN],
+                    pair * PAIR % GATE_RUN,
+                    pair == 0,
                     False,
-                    pair == X_GROUPS // PAIR - 1,
                 )
-            if s + 2 < X_STAGES:
-                quantise_x_stage(s + 2)
-            quarter = slice(s * H // X_STAGES, (s + 1) * H // X_STAGES)
-            nc.vector.reciprocal(out=tau_p[:, quarter], in_=tau_p[:, quarter])
+                if pair == 2 * s:
+                    groups = STAGE if s + 1 < X_STAGES else H_GROUPS
+                    quantised.extend(
+                        transpose_and_quantise(nc, pools, ident, raw[s + 1], groups, "x%d" % (s + 1))
+                    )
+                    quarter = slice(s * H // X_STAGES, (s + 1) * H // X_STAGES)
+                    nc.vector.scalar_tensor_tensor(
+                        out=inv_tau_p[:, quarter],
+                        in0=log_term[:, quarter],
+                        scalar=1.0,
+                        in1=relu_tau[:, quarter],
+                        op0=ALU.add,
+                        op1=ALU.add,
+                    )
+                    nc.vector.reciprocal(out=inv_tau_p[:, quarter], in_=inv_tau_p[:, quarter])
+        multiply_pair(
+            nc,
+            pre_acc,
+            quantised[X_PAIRS],
+            gate_words[X_PAIRS],
+            gate_planes[1],
+            X_GROUPS - GATE_RUN,
+            False,
+            True,
+        )
 
-        rest = keep.tile([P, ROW_TILES, H], F32)
-        for b in range(ROW_TILES):
-            nc.vector.scalar_tensor_tensor(
-                out=rest[:, b, :],
-                in0=h_raw[:, b, :],
-                scalar=-1.0,
-                in1=tau_p[:],
-                op0=ALU.mult,
-                op1=ALU.mult,
-            )
-        all_banks = [(b, half) for b in range(ROW_TILES) for half in range(COL_HALVES)]
-        gate = {}
-        for b, half in all_banks:
-            gate[b, half] = work.tile([P, N_PASS], F32, tag="gate", name="gate")
+        rec_acc = four_tiles(banks, "bank", "rec_acc")
+        multiply_pair(nc, rec_acc, quantised[X_PAIRS], rec_words, rec_planes, 0, True, True)
+
+        gate = four_tiles(work, "gate", "gate")
+        rest = four_tiles(work, "rest", "rest")
+        for b, half in BANKS:
             nc.vector.tensor_tensor(
                 out=gate[b, half][:],
-                in0=pre_acc[b][half][:],
+                in0=pre_acc[b, half][:],
                 in1=bias_all[:, bank_columns(half)],
                 op=ALU.add,
             )
-        for b, half in all_banks:
+        for b, half in BANKS:
             nc.scalar.activation(out=gate[b, half][:], in_=gate[b, half][:], func=ACT.Tanh)
             nc.scalar.activation(out=gate[b, half][:], in_=gate[b, half][:], func=ACT.Sigmoid)
-        for b, half in all_banks:
+            nc.vector.scalar_tensor_tensor(
+                out=rest[b, half][:],
+                in0=h_raw[:, b, bank_columns(half)],
+                scalar=-1.0,
+                in1=inv_tau_p[:, bank_columns(half)],
+                op0=ALU.mult,
+                op1=ALU.mult,
+            )
+        for b, half in BANKS:
             nc.vector.tensor_tensor(
-                out=gate[b, half][:],
-                in0=gate[b, half][:],
-                in1=rec[:, b, bank_columns(half)],
-                op=ALU.mult,
+                out=gate[b, half][:], in0=gate[b, half][:], in1=rec_acc[b, half][:], op=ALU.mult
             )
             nc.vector.tensor_tensor(
-                out=rest[:, b, bank_columns(half)],
-                in0=gate[b, half][:],
-                in1=rest[:, b, bank_columns(half)],
-                op=ALU.add,
+                out=rest[b, half][:], in0=gate[b, half][:], in1=rest[b, half][:], op=ALU.add
             )
 
-        in_acc = four_banks(banks, "in_acc")
-        for pair in range(X_GROUPS // PAIR):
+        in_acc = four_tiles(sums, "bank", "in_acc")
+        for pair in range(X_PAIRS):
             multiply_pair(
                 nc,
                 in_acc,
-                codes,
-                code_scales,
-                pair * PAIR,
+                quantised[pair],
                 in_words[pair],
                 in_planes,
                 pair * PAIR,
                 pair == 0,
-                pair == X_GROUPS // PAIR - 1,
+                pair == X_PAIRS - 1,
             )
-        for b, half in all_banks:
+        x_in = four_tiles(work, "x_in", "x_in")
+        for b, half in BANKS:
             rows = slice(b * P, (b + 1) * P)
-            x_in = work.tile([P, N_PASS], F32, tag="x_in")
-            nc.scalar.copy(out=x_in[:], in_=in_acc[b][half][:])
-            nc.sync.dma_start(out=out_0[rows, bank_columns(half)], in_=x_in[:])
+            nc.scalar.copy(out=x_in[b, half][:], in_=in_acc[b, half][:])
+            nc.sync.dma_start(out=out_0[rows, bank_columns(half)], in_=x_in[b, half][:])
             nc.vector.tensor_tensor(
-                out=rest[:, b, bank_columns(half)],
-                in0=x_in[:],
-                in1=rest[:, b, bank_columns(half)],
-                op=ALU.add,
+                out=rest[b, half][:], in0=x_in[b, half][:], in1=rest[b, half][:], op=ALU.add
             )
-            nc.sync.dma_start(out=out_1[rows, bank_columns(half)], in_=rest[:, b, bank_columns(half)])
+            nc.sync.dma_start(out=out_1[rows, bank_columns(half)], in_=rest[b, half][:])

@@ -26,6 +26,7 @@ STAGE = 4
 X_STAGES = X_GROUPS // STAGE
 WORDS = K_PASS // 2
 GATE_RUN = 8
+JOINT_PAIRS = 4
 WEIGHT_BUFFERS = 12
 
 FLOPS = 2 * B * (2 * IN * H + 2 * H * H)
@@ -95,9 +96,9 @@ def transpose_and_quantise(nc, pools, ident, raw, groups, name):
     return quantised
 
 
-def multiply_pair(nc, acc, quantised, words, planes, group, start, stop):
+def multiply_pair(nc, acc, quantised, words, planes, group, start, stop, bank_list=BANKS):
     codes, scales = quantised
-    for b, half in BANKS:
+    for b, half in bank_list:
         rows = slice(b * P, (b + 1) * P)
         for i in range(PAIR):
             nc.tensor.matmul_mx(
@@ -272,7 +273,9 @@ def tile_ltccell_pa_k_kernel(
             )
         for b, half in BANKS:
             nc.scalar.activation(out=gate[b, half][:], in_=gate[b, half][:], func=ACT.Tanh)
-            nc.scalar.activation(out=gate[b, half][:], in_=gate[b, half][:], func=ACT.Sigmoid)
+            nc.scalar.activation(
+                out=gate[b, half][:], in_=gate[b, half][:], func=ACT.Tanh, scale=0.5
+            )
             nc.vector.scalar_tensor_tensor(
                 out=rest[b, half][:],
                 in0=h_raw[:, b, bank_columns(half)],
@@ -282,15 +285,27 @@ def tile_ltccell_pa_k_kernel(
                 op1=ALU.mult,
             )
         for b, half in BANKS:
-            nc.vector.tensor_tensor(
-                out=gate[b, half][:], in0=gate[b, half][:], in1=rec_acc[b, half][:], op=ALU.mult
+            nc.vector.scalar_tensor_tensor(
+                out=gate[b, half][:],
+                in0=gate[b, half][:],
+                scalar=1.0,
+                in1=rec_acc[b, half][:],
+                op0=ALU.add,
+                op1=ALU.mult,
             )
-            nc.vector.tensor_tensor(
-                out=rest[b, half][:], in0=gate[b, half][:], in1=rest[b, half][:], op=ALU.add
+            nc.vector.scalar_tensor_tensor(
+                out=rest[b, half][:],
+                in0=gate[b, half][:],
+                scalar=0.5,
+                in1=rest[b, half][:],
+                op0=ALU.mult,
+                op1=ALU.add,
             )
 
         in_acc = four_tiles(sums, "bank", "in_acc")
-        for pair in range(X_PAIRS):
+        x_in = four_tiles(work, "x_in", "x_in")
+
+        def add_x_pair(pair, bank_list):
             multiply_pair(
                 nc,
                 in_acc,
@@ -300,9 +315,14 @@ def tile_ltccell_pa_k_kernel(
                 pair * PAIR,
                 pair == 0,
                 pair == X_PAIRS - 1,
+                bank_list,
             )
-        x_in = four_tiles(work, "x_in", "x_in")
+
+        for pair in range(JOINT_PAIRS):
+            add_x_pair(pair, BANKS)
         for b, half in BANKS:
+            for pair in range(JOINT_PAIRS, X_PAIRS):
+                add_x_pair(pair, [(b, half)])
             rows = slice(b * P, (b + 1) * P)
             nc.scalar.copy(out=x_in[b, half][:], in_=in_acc[b, half][:])
             nc.sync.dma_start(out=out_0[rows, bank_columns(half)], in_=x_in[b, half][:])

@@ -42,13 +42,18 @@ def scale_planes(nc, pool, groups, name):
     return planes
 
 
-def load_scale_rows(nc, planes, scales, first, count):
-    for q in range(8):
-        partition = 32 * (q // 4) + q % 4
-        nc.sync.dma_start(
-            out=planes[partition:P:64, :, :].bitcast(I32),
-            in_=scales[first : first + count, q:16:8, :].bitcast(I32).rearrange("g q n -> q g n"),
-        )
+def load_scale_rows(nc, planes, scales, first, count, parts=1):
+    size = count // parts
+    for part in range(parts):
+        at = part * size
+        for q in range(8):
+            partition = 32 * (q // 4) + q % 4
+            nc.sync.dma_start(
+                out=planes[partition:P:64, at : at + size, :].bitcast(I32),
+                in_=scales[first + at : first + at + size, q:16:8, :]
+                .bitcast(I32)
+                .rearrange("g q n -> q g n"),
+            )
 
 
 def load_weight_pair(nc, pool, words, pair, name):
@@ -187,7 +192,7 @@ def tile_ltccell_pa_k_kernel(
             gate_words.append(load_weight_pair(nc, weights, gate_w_words, 2 * s + 1, "gate_words"))
         gate_words.append(load_weight_pair(nc, weights, gate_w_words, X_PAIRS, "gate_words"))
         rec_words = load_weight_pair(nc, weights, W_rec_words, 0, "rec_words")
-        load_scale_rows(nc, in_planes, W_in_scales, 0, X_GROUPS)
+        load_scale_rows(nc, in_planes, W_in_scales, 0, X_GROUPS, 2)
         in_words = [
             load_weight_pair(nc, weights, W_in_words, pair, "in_words") for pair in range(X_PAIRS)
         ]

import concourse.mybir as mybir
from concourse.masks import make_identity

F32 = mybir.dt.float32
BF16 = mybir.dt.bfloat16
I32 = mybir.dt.int32
U32 = mybir.dt.uint32
U8 = mybir.dt.uint8
FP8X4 = mybir.dt.float8_e4m3fn_x4
FP4X4 = mybir.dt.float4_e2m1fn_x4
ACT = mybir.ActivationFunctionType
ALU = mybir.AluOpType

P = 128
B, IN, H = 256, 8192, 1024
K_PASS = 4 * P
N_PASS = 512
ROW_TILES = B // P
COL_HALVES = H // N_PASS
BANKS = [(b, half) for b in range(ROW_TILES) for half in range(COL_HALVES)]
X_GROUPS = IN // K_PASS
H_GROUPS = H // K_PASS
PAIR = 2
X_PAIRS = X_GROUPS // PAIR
STAGE = 4
X_STAGES = X_GROUPS // STAGE
WORDS = K_PASS // 2
GATE_RUN = 8
JOINT_PAIRS = 4
WEIGHT_BUFFERS = 12

FLOPS = 2 * B * (2 * IN * H + 2 * H * H)


def bank_columns(half):
    return slice(half * N_PASS, (half + 1) * N_PASS)


def scale_planes(nc, pool, groups, name):
    planes = pool.tile([P, groups, H], U8, name=name, align_bytes=64)
    nc.vector.memset(planes[:].bitcast(I32), 0)
    return planes


def load_scale_rows(nc, planes, scales, first, count, parts=1):
    size = count // parts
    for part in range(parts):
        at = part * size
        for q in range(8):
            partition = 32 * (q // 4) + q % 4
            nc.sync.dma_start(
                out=planes[partition:P:64, at : at + size, :].bitcast(I32),
                in_=scales[first + at : first + at + size, q:16:8, :]
                .bitcast(I32)
                .rearrange("g q n -> q g n"),
            )


def load_weight_pair(nc, pool, words, pair, name):
    tile = pool.tile([P, PAIR, 2 * H], U8, tag="words", name=name, align_bytes=64)
    nc.sync.dma_start(
        out=tile[:].bitcast(I32),
        in_=words[PAIR * pair : PAIR * (pair + 1)].bitcast(I32).rearrange("g p n -> p g n"),
    )
    return tile


def transpose_and_quantise(nc, pools, ident, raw, groups, name):
    keep, regroup, banks = pools
    raw_words = raw[:].bitcast(F32)
    grouped = []
    for pair in range(groups // PAIR):
        grouped.append(regroup.tile([P, PAIR, 4 * B], BF16, tag="grouped", name="grouped", align_bytes=64))
        for i in range(PAIR):
            g = pair * PAIR + i
            bank = banks.tile([P, N_PASS], F32, tag="bank", name="transposed")
            for b in range(ROW_TILES):
                for u in range(2):
                    nc.tensor.transpose(
                        bank[:, (2 * b + u) * P : (2 * b + u + 1) * P],
                        raw_words[:, b, g * WORDS + u : (g + 1) * WORDS : 2],
                        ident[:],
                    )
            copy = nc.vector.tensor_copy if i == 0 else nc.scalar.copy
            copy(
                out=grouped[pair][:, i, :]
                .bitcast(F32)
                .rearrange("p (b r u) -> p b r u", b=ROW_TILES, u=2),
                in_=bank[:].rearrange("p (b u r) -> p b r u", b=ROW_TILES, u=2),
            )
    quantised = []
    for pair in range(groups // PAIR):
        codes = keep.tile([P, PAIR, B], U32, name="%s_codes%d" % (name, pair), align_bytes=64)
        scales = keep.tile([P, PAIR, B], U8, name="%s_scales%d" % (name, pair), align_bytes=64)
        nc.vector.quantize_mx(
            out=codes[:].rearrange("p g c -> p (g c)").bitcast(FP8X4),
            scales=scales[:].rearrange("p g c -> p (g c)"),
            in_=grouped[pair][:].rearrange("p g c -> p (g c)"),
        )
        quantised.append((codes, scales))
    return quantised


def multiply_pair(nc, acc, quantised, words, planes, group, start, stop, bank_list=BANKS):
    codes, scales = quantised
    for b, half in bank_list:
        rows = slice(b * P, (b + 1) * P)
        for i in range(PAIR):
            nc.tensor.matmul_mx(
                out=acc[b, half][:],
                lhsT=codes[:, i, rows].bitcast(FP8X4),
                lhsT_scale=scales[:, i, rows],
                rhs=words[:, i, 2 * half * N_PASS : 2 * (half + 1) * N_PASS].bitcast(FP4X4),
                rhs_scale=planes[:, group + i, bank_columns(half)],
                start=start and i == 0,
                stop=stop and i == PAIR - 1,
            )


def four_tiles(pool, tag, name):
    return dict(
        ((b, half), pool.tile([P, N_PASS], F32, tag=tag, name="%s%d%d" % (name, b, half)))
        for b, half in BANKS
    )


def tile_ltccell_pa_k_kernel(
    tc,
    x,
    h,
    tau,
    W_in_words,
    W_in_scales,
    W_rec_words,
    W_rec_scales,
    gate_w_words,
    gate_w_scales,
    gate_b,
    out_0,
    out_1,
):
    nc = tc.nc
    x_rows = x.rearrange("(b p) k -> p b k", p=P)
    h_rows = h.rearrange("(b p) k -> p b k", p=P)

    with (
        tc.tile_pool(name="keep", bufs=1) as keep,
        tc.tile_pool(name="weights", bufs=WEIGHT_BUFFERS) as weights,
        tc.tile_pool(name="regroup", bufs=4) as regroup,
        tc.tile_pool(name="work", bufs=len(BANKS)) as work,
        tc.psum_pool(name="banks", bufs=4) as banks,
        tc.psum_pool(name="sums", bufs=4) as sums,
        tc.manual_schedule(),
    ):
        gate_planes = [scale_planes(nc, keep, GATE_RUN, "gate_planes0")]
        vectors = keep.tile([P, 2 * H], BF16)
        nc.vector.memset(vectors[:].bitcast(I32), 0)
        nc.scalar.dma_start(out=vectors[0:1, 0:H], in_=tau.rearrange("(o n) -> o n", o=1))
        nc.scalar.dma_start(out=vectors[0:1, H : 2 * H], in_=gate_b.rearrange("(o n) -> o n", o=1))
        ones = keep.tile([P, P], BF16)
        nc.vector.memset(ones[:], 1.0)
        gate_planes.append(
            scale_planes(nc, keep, X_GROUPS + H_GROUPS - GATE_RUN, "gate_planes1")
        )
        rec_planes = scale_planes(nc, keep, H_GROUPS, "rec_planes")
        in_planes = scale_planes(nc, keep, X_GROUPS, "in_planes")
        ident = keep.tile([P, P], F32)
        make_identity(nc, ident[:])

        def load_rows(rows, first, count, name):
            tile = keep.tile([P, ROW_TILES, count * K_PASS], BF16, name=name)
            nc.sync.dma_start(
                out=tile[:], in_=rows[:, :, first * K_PASS : (first + count) * K_PASS]
            )
            return tile

        raw = [load_rows(x_rows, 0, STAGE, "x_raw0")]
        gate_words = []
        for s in range(X_STAGES):
            if s * STAGE == 0:
                load_scale_rows(nc, gate_planes[0], gate_w_scales, 0, GATE_RUN)
            if s * STAGE == GATE_RUN:
                load_scale_rows(
                    nc, gate_planes[1], gate_w_scales, GATE_RUN, X_GROUPS + H_GROUPS - GATE_RUN
                )
                load_scale_rows(nc, rec_planes, W_rec_scales, 0, H_GROUPS)
            gate_words.append(load_weight_pair(nc, weights, gate_w_words, 2 * s, "gate_words"))
            if s + 1 < X_STAGES:
                raw.append(load_rows(x_rows, (s + 1) * STAGE, STAGE, "x_raw%d" % (s + 1)))
            else:
                raw.append(load_rows(h_rows, 0, H_GROUPS, "h_raw"))
            gate_words.append(load_weight_pair(nc, weights, gate_w_words, 2 * s + 1, "gate_words"))
        gate_words.append(load_weight_pair(nc, weights, gate_w_words, X_PAIRS, "gate_words"))
        rec_words = load_weight_pair(nc, weights, W_rec_words, 0, "rec_words")
        load_scale_rows(nc, in_planes, W_in_scales, 0, X_GROUPS, 2)
        in_words = [
            load_weight_pair(nc, weights, W_in_words, pair, "in_words") for pair in range(X_PAIRS)
        ]
        h_raw = raw[X_STAGES]

        pools = (keep, regroup, banks)
        quantised = transpose_and_quantise(nc, pools, ident, raw[0], STAGE, "x0")

        spread = four_tiles(sums, "bank", "spread")
        relu_tau = keep.tile([P, H], F32)
        log_term = keep.tile([P, H], F32)
        bias_all = keep.tile([P, H], F32)
        for vector, half in BANKS:
            nc.tensor.matmul(
                spread[vector, half][:],
                lhsT=ones[:],
                rhs=vectors[:, vector * H + half * N_PASS : vector * H + (half + 1) * N_PASS],
                start=True,
                stop=True,
            )
        for half in range(COL_HALVES):
            nc.scalar.activation(
                out=log_term[:, bank_columns(half)], in_=spread[0, half][:], func=ACT.Abs
            )
            nc.scalar.activation(
                out=relu_tau[:, bank_columns(half)], in_=spread[0, half][:], func=ACT.Relu
            )
            nc.vector.tensor_copy(out=bias_all[:, bank_columns(half)], in_=spread[1, half][:])
        nc.scalar.activation(out=log_term[:], in_=log_term[:], func=ACT.Exp, scale=-1.0)
        nc.scalar.activation(out=log_term[:], in_=log_term[:], func=ACT.Ln, bias=1.0)

        pre_acc = four_tiles(sums, "bank", "pre_acc")
        inv_tau_p = keep.tile([P, H], F32)
        for s in range(X_STAGES):
            for pair in (2 * s, 2 * s + 1):
                multiply_pair(
                    nc,
                    pre_acc,
                    quantised[pair],
                    gate_words[pair],
                    gate_planes[pair * PAIR // GATE_RUN],
                    pair * PAIR % GATE_RUN,
                    pair == 0,
                    False,
                )
                if pair == 2 * s:
                    groups = STAGE if s + 1 < X_STAGES else H_GROUPS
                    quantised.extend(
                        transpose_and_quantise(nc, pools, ident, raw[s + 1], groups, "x%d" % (s + 1))
                    )
                    quarter = slice(s * H // X_STAGES, (s + 1) * H // X_STAGES)
                    nc.vector.scalar_tensor_tensor(
                        out=inv_tau_p[:, quarter],
                        in0=log_term[:, quarter],
                        scalar=1.0,
                        in1=relu_tau[:, quarter],
                        op0=ALU.add,
                        op1=ALU.add,
                    )
                    nc.vector.reciprocal(out=inv_tau_p[:, quarter], in_=inv_tau_p[:, quarter])
        multiply_pair(
            nc,
            pre_acc,
            quantised[X_PAIRS],
            gate_words[X_PAIRS],
            gate_planes[1],
            X_GROUPS - GATE_RUN,
            False,
            True,
        )

        rec_acc = four_tiles(banks, "bank", "rec_acc")
        multiply_pair(nc, rec_acc, quantised[X_PAIRS], rec_words, rec_planes, 0, True, True)

        gate = four_tiles(work, "gate", "gate")
        rest = four_tiles(work, "rest", "rest")
        for b, half in BANKS:
            nc.vector.tensor_tensor(
                out=gate[b, half][:],
                in0=pre_acc[b, half][:],
                in1=bias_all[:, bank_columns(half)],
                op=ALU.add,
            )
        for b, half in BANKS:
            nc.scalar.activation(out=gate[b, half][:], in_=gate[b, half][:], func=ACT.Tanh)
            nc.scalar.activation(
                out=gate[b, half][:], in_=gate[b, half][:], func=ACT.Tanh, scale=0.5
            )
            nc.vector.scalar_tensor_tensor(
                out=rest[b, half][:],
                in0=h_raw[:, b, bank_columns(half)],
                scalar=-1.0,
                in1=inv_tau_p[:, bank_columns(half)],
                op0=ALU.mult,
                op1=ALU.mult,
            )
        for b, half in BANKS:
            nc.vector.scalar_tensor_tensor(
                out=gate[b, half][:],
                in0=gate[b, half][:],
                scalar=1.0,
                in1=rec_acc[b, half][:],
                op0=ALU.add,
                op1=ALU.mult,
            )
            nc.vector.scalar_tensor_tensor(
                out=rest[b, half][:],
                in0=gate[b, half][:],
                scalar=0.5,
                in1=rest[b, half][:],
                op0=ALU.mult,
                op1=ALU.add,
            )

        in_acc = four_tiles(sums, "bank", "in_acc")
        x_in = four_tiles(work, "x_in", "x_in")

        def add_x_pair(pair, bank_list):
            multiply_pair(
                nc,
                in_acc,
                quantised[pair],
                in_words[pair],
                in_planes,
                pair * PAIR,
                pair == 0,
                pair == X_PAIRS - 1,
                bank_list,
            )

        for pair in range(JOINT_PAIRS):
            add_x_pair(pair, BANKS)
        for b, half in BANKS:
            for pair in range(JOINT_PAIRS, X_PAIRS):
                add_x_pair(pair, [(b, half)])
            rows = slice(b * P, (b + 1) * P)
            nc.scalar.copy(out=x_in[b, half][:], in_=in_acc[b, half][:])
            nc.sync.dma_start(out=out_0[rows, bank_columns(half)], in_=x_in[b, half][:])
            nc.vector.tensor_tensor(
                out=rest[b, half][:], in0=x_in[b, half][:], in1=rest[b, half][:], op=ALU.add
            )
            nc.sync.dma_start(out=out_1[rows, bank_columns(half)], in_=rest[b, half][:])
